import numpy as np
import ml_dtypes


def mxq(x, axis, fmt="e4m3"):
    dtype, down = {"e4m3": (ml_dtypes.float8_e4m3fn, 7), "e5m2": (ml_dtypes.float8_e5m2, 14)}[fmt]
    v = np.moveaxis(np.asarray(x, np.float32).astype(ml_dtypes.bfloat16).astype(np.float64), axis, -1)
    blocks = v.reshape(v.shape[:-1] + (-1, 32))
    amax = np.abs(blocks).max(-1, keepdims=True)
    byte = np.maximum(np.where(amax > 0, np.frexp(amax)[1] - 1 + 127, 0) - down, 1)
    scale = np.exp2(byte - 127.0)
    codes = (blocks / scale).astype(np.float32).astype(dtype).astype(np.float64)
    return np.moveaxis((codes * scale).reshape(v.shape), -1, axis)


WIDE = False


def mx_kscale(k):
    if not WIDE:
        return np.ones(k)
    levels = np.array([10, -10, 5, -5, 0])
    a = np.random.permutation(np.resize(levels, k // 512 * 4)).reshape(k // 512, 4)
    idx = np.arange(k)
    return np.exp2(a[idx // 512, idx % 128 // 32])


BF16 = ml_dtypes.bfloat16


def bf(x):
    return np.asarray(x, np.float32).astype(BF16)


def f64(x):
    return np.asarray(x).astype(np.float64)


B, C, HH, WW, HD = 1, 1024, 32, 32, 128
S = HH * WW
NH = C // HD
EPS = 1e-4


def mp_weight(w):
    o, i, kh, kw = w.shape
    fan_in = i * kh * kw
    n = np.sqrt(np.sum(w * w, axis=(1, 2, 3), keepdims=True))
    alpha = 1.0 / np.sqrt(fan_in)
    wn = w / (EPS + alpha * n) / np.sqrt(fan_in)
    return wn[:, :, 0, 0]


def pixel_norm(t):
    return t * (1.0 / np.sqrt(np.mean(t * t, axis=1, keepdims=True) + EPS))


def to_heads(t):
    return t.reshape(B, S, NH, HD).transpose(0, 2, 1, 3)


def setup_inputs():
    s = mx_kscale(C)
    sc = s * np.sqrt(np.mean(1.0 / s**2))
    gain = 0.002 * np.exp2(np.random.uniform(-2.0, 2.0, 3 * C))
    return {"x": bf(np.random.standard_normal((B, C, HH, WW)) * 0.06 * sc[None, :, None, None]),
            "w_attn": bf(np.random.standard_normal((3 * C, C, 1, 1)) * gain[:, None, None, None] / sc[None, :, None, None])}


def reference(x, w_attn):
    wn = mp_weight(f64(w_attn))
    xt = f64(x).reshape(B, C, S).transpose(0, 2, 1)
    p = mxq(xt, 2, "e4m3") @ mxq(wn.T, 0, "e4m3")
    q, k, v = np.split(p, 3, axis=-1)
    return pixel_norm(to_heads(q)), pixel_norm(to_heads(k)), pixel_norm(to_heads(v))

@@ -1,0 +1,287 @@
+import math
+from contextlib import ExitStack
+
+import concourse.masks as masks
+import concourse.mybir as mybir
+
+F32 = mybir.dt.float32
+BF16 = mybir.dt.bfloat16
+U32 = mybir.dt.uint32
+U8 = mybir.dt.uint8
+FP8X4 = mybir.dt.float8_e4m3fn_x4
+ACT = mybir.ActivationFunctionType
+ALU = mybir.AluOpType
+
+P = 128
+PACK = 4
+CHANNELS = 1024
+PASSES = CHANNELS // (P * PACK)
+POSITIONS = 1024
+HEADS = 8
+HEAD_DIM = 128
+THIRDS = 3
+EPS = 1e-4
+NORM_FLOOR = EPS * math.sqrt(CHANNELS)
+BANK = 512
+HEADS_PER_BANK = BANK // HEAD_DIM
+BANKS_PER_GROUP = HEADS // HEADS_PER_BANK
+
+BLOCKS = THIRDS * HEADS
+S_RUN = 4
+S_SPAN = P * S_RUN
+SPANS = POSITIONS // S_SPAN
+GROUPS_PER_THIRD = POSITIONS // P
+GROUPS = THIRDS * GROUPS_PER_THIRD
+BLOCK_STEPS = 4
+FIRST_PRODUCT_STEP = HEADS - 1 + BLOCK_STEPS - 1
+
+FLOPS = 2 * POSITIONS * CHANNELS * THIRDS * HEADS * HEAD_DIM
+
+
+def tile_cosineattention_pa_kernel(tc, x, w_attn, out_0, out_1, out_2):
+    nc = tc.nc
+    x_rows = x.rearrange("b c h w -> (b c) (h w)")
+    w_rows = w_attn.rearrange("o i a b -> o (i a b)")
+    outs = [o.rearrange("b n s d -> (b n) s d") for o in (out_0, out_1, out_2)]
+
+    with ExitStack() as ctx:
+        ctx.enter_context(tc.manual_schedule())
+        keep = ctx.enter_context(tc.tile_pool(name="keep", bufs=1))
+        x_stage = ctx.enter_context(tc.tile_pool(name="x_stage", bufs=2))
+        w_stage = ctx.enter_context(tc.tile_pool(name="w_stage", bufs=3))
+        tiny = ctx.enter_context(tc.tile_pool(name="tiny", bufs=4))
+        norm = ctx.enter_context(tc.tile_pool(name="norm", bufs=3))
+        results = ctx.enter_context(tc.tile_pool(name="results", bufs=3))
+        psum = ctx.enter_context(tc.psum_pool(name="psum", bufs=2))
+
+        identity = keep.tile([P, P], F32)
+        zero_column = keep.tile([P, 1], F32)
+        eps_column = keep.tile([P, 1], F32)
+        table_warmer = keep.tile([P, 1], F32)
+        half_column = keep.tile([P, 1], F32)
+        minus_one_column = keep.tile([P, 1], F32)
+        x_raw = keep.tile([P, PASSES * PACK, POSITIONS], BF16)
+        x_codes = keep.tile([P, PASSES, POSITIONS], U32, align_bytes=64)
+        x_scales = keep.tile([P, PASSES, POSITIONS], U8, align_bytes=64)
+        w_raw = keep.tile([P, BLOCKS, CHANNELS], BF16)
+        w_codes = keep.tile([P, BLOCKS // HEADS_PER_BANK, PASSES, BANK], U32, align_bytes=64)
+        w_scales = keep.tile([P, BLOCKS // HEADS_PER_BANK, PASSES, BANK], U8, align_bytes=64)
+
+        small_bank = psum.tile([P, 2, P], F32, tag="small", bufs=1)
+        head_sum_turned = small_bank[:, 0, :]
+        inv_rms_bank = small_bank[:, 1, :]
+
+        sum_squares = {}
+        filter_scales = {}
+        normed = {}
+        turned = {}
+        grouped_w = {}
+        grouped_x = {}
+        products = {}
+        squares = {}
+        inv_rms_turned = {}
+        inv_rms = {}
+        result = {}
+
+        def load_everything():
+            for b in range(BLOCKS):
+                nc.sync.dma_start(out=w_raw[:, b, :], in_=w_rows[P * b : P * (b + 1), :])
+                if b < PASSES * 2:
+                    nc.sync.dma_start(
+                        out=x_raw[:, 2 * b : 2 * b + 2, :],
+                        in_=x_rows[2 * P * b : 2 * P * (b + 1), :].rearrange("(p e) s -> p e s", e=2),
+                    )
+
+        def regroup_x(unit):
+            g, span = divmod(unit, SPANS)
+            grouped = x_stage.tile([P, S_RUN, P, PACK], BF16, align_bytes=64)
+            nc.vector.tensor_copy(
+                out=grouped[:],
+                in_=x_raw[:, PACK * g : PACK * (g + 1), S_SPAN * span : S_SPAN * (span + 1)].rearrange(
+                    "p t (m q) -> p q m t", q=S_RUN
+                ),
+            )
+            grouped_x[unit] = grouped
+
+        def quantise_x(unit):
+            g, span = divmod(unit, SPANS)
+            columns = slice(S_SPAN * span, S_SPAN * (span + 1))
+            nc.vector.quantize_mx(
+                out=x_codes[:, g, columns].bitcast(FP8X4),
+                scales=x_scales[:, g, columns],
+                in_=grouped_x[unit][:].rearrange("p q m t -> p (q m t)"),
+            )
+
+        def filter_sum_squares(b):
+            unread = w_stage.tile([P, CHANNELS], BF16)
+            total = tiny.tile([P, 1], F32)
+            nc.scalar.activation(out=unread[:], in_=w_raw[:, b, :], func=ACT.Square, accum_out=total[:])
+            sum_squares[b] = total
+
+        def filter_scale(b):
+            length = tiny.tile([P, 1], F32)
+            nc.gpsimd.tensor_tensor(out=length[:], in0=sum_squares[b][:], in1=half_column[:], op=ALU.pow)
+            padded = tiny.tile([P, 1], F32)
+            nc.gpsimd.tensor_scalar_add(out=padded[:], in0=length[:], scalar1=NORM_FLOOR)
+            scale = tiny.tile([P, 1], F32)
+            nc.gpsimd.tensor_tensor(out=scale[:], in0=padded[:], in1=minus_one_column[:], op=ALU.pow)
+            filter_scales[b] = scale
+
+        def normalise_filters(b):
+            wn = w_stage.tile([P, CHANNELS], BF16)
+            nc.vector.tensor_scalar_mul(out=wn[:], in0=w_raw[:, b, :], scalar1=filter_scales[b][:])
+            normed[b] = wn
+
+        def transpose_filters(b):
+            words = normed[b][:].bitcast(F32)
+            bank = psum.tile([P, PASSES * 2, P], F32, tag="turned", bufs=1)
+            for c in range(PASSES * 2):
+                nc.tensor.transpose(bank[:, c, :], words[:, P * c : P * (c + 1)], identity[:])
+            turned[b] = bank
+
+        def regroup_filters(b):
+            grouped = w_stage.tile([P, PASSES, P, PACK], BF16, align_bytes=64)
+            copy = nc.scalar.copy if b < HEADS else nc.vector.tensor_copy
+            copy(
+                out=grouped[:]
+                .rearrange("p g o t -> p (g o t)")
+                .bitcast(F32)
+                .rearrange("p (g o u) -> p g o u", g=PASSES, u=2),
+                in_=turned[b][:].rearrange("p (g u) o -> p g o u", u=2),
+            )
+            grouped_w[b] = grouped
+
+        def quantise_filters(b):
+            bank, head = divmod(b, HEADS_PER_BANK)
+            columns = slice(HEAD_DIM * head, HEAD_DIM * (head + 1))
+            for g in range(PASSES):
+                nc.vector.quantize_mx(
+                    out=w_codes[:, bank, g, columns].bitcast(FP8X4),
+                    scales=w_scales[:, bank, g, columns],
+                    in_=grouped_w[b][:, g].rearrange("p o t -> p (o t)"),
+                )
+
+        def project(q):
+            third, block = divmod(q, GROUPS_PER_THIRD)
+            columns = slice(P * block, P * (block + 1))
+            banks = []
+            for h in range(BANKS_PER_GROUP):
+                bank = psum.tile([P, BANK], F32, tag="product", bufs=6)
+                for g in range(PASSES):
+                    nc.tensor.matmul_mx(
+                        out=bank[:],
+                        lhsT=x_codes[:, g, columns].bitcast(FP8X4),
+                        lhsT_scale=x_scales[:, g, columns],
+                        rhs=w_codes[:, BANKS_PER_GROUP * third + h, g, :].bitcast(FP8X4),
+                        rhs_scale=w_scales[:, BANKS_PER_GROUP * third + h, g, :],
+                        start=(g == 0),
+                        stop=(g == PASSES - 1),
+                    )
+                banks.append(bank)
+            products[q] = banks
+
+        def square_products(q):
+            sq = norm.tile([P, HEADS * HEAD_DIM], F32)
+            for h in range(BANKS_PER_GROUP):
+                nc.scalar.activation(out=sq[:, BANK * h : BANK * (h + 1)], in_=products[q][h][:], func=ACT.Square)
+            squares[q] = sq
+
+        def sum_over_heads(q):
+            for n in range(HEADS):
+                nc.tensor.matmul(
+                    out=head_sum_turned,
+                    lhsT=squares[q][:, HEAD_DIM * n : HEAD_DIM * (n + 1)],
+                    rhs=identity[:],
+                    is_transpose=True,
+                    start=(n == 0),
+                    stop=(n == HEADS - 1),
+                )
+
+        def inverse_rms(q):
+            r_turned = norm.tile([P, P], F32)
+            nc.scalar.activation(
+                out=r_turned[:], in_=head_sum_turned, func=ACT.Abs_reciprocal_sqrt, scale=1.0 / HEADS, bias=eps_column[:]
+            )
+            inv_rms_turned[q] = r_turned
+
+        def turn_inverse_rms_back(q):
+            nc.tensor.transpose(inv_rms_bank, inv_rms_turned[q][:], identity[:])
+
+        def fetch_inverse_rms(q):
+            r = norm.tile([P, HEAD_DIM], F32)
+            nc.scalar.copy(out=r[:], in_=inv_rms_bank)
+            inv_rms[q] = r
+
+        def scale_and_store(q):
+            third, block = divmod(q, GROUPS_PER_THIRD)
+            span, run = divmod(block, S_RUN)
+            if run == 0:
+                result[0] = results.tile([P, HEADS, S_RUN, HEAD_DIM], F32, name="res")
+            res = result[0]
+            for h in range(BANKS_PER_GROUP):
+                heads = slice(HEADS_PER_BANK * h, HEADS_PER_BANK * (h + 1))
+                nc.vector.tensor_tensor(
+                    out=res[:, heads, run, :],
+                    in0=products[q][h][:].rearrange("p (n d) -> p n d", n=HEADS_PER_BANK),
+                    in1=inv_rms[q][:].unsqueeze(1).to_broadcast([P, HEADS_PER_BANK, HEAD_DIM]),
+                    op=ALU.mult,
+                )
+                if run == S_RUN - 1:
+                    nc.sync.dma_start(
+                        out=outs[third][heads, S_SPAN * span : S_SPAN * (span + 1), :].rearrange(
+                            "n (m q) d -> m n (q d)", q=S_RUN
+                        ),
+                        in_=res[:, heads, :, :].rearrange("m n q d -> m n (q d)"),
+                    )
+
+        load_everything()
+        nc.vector.memset(zero_column[:], 0.0)
+        nc.vector.tensor_scalar_add(out=eps_column[:], in0=zero_column[:], scalar1=EPS)
+        nc.vector.memset(half_column[:], 0.5)
+        nc.vector.memset(minus_one_column[:], -1.0)
+        nc.scalar.activation(out=table_warmer[:], in_=eps_column[:], func=ACT.Abs_reciprocal_sqrt)
+        masks.make_identity(nc, identity[:])
+
+        def is_block(b):
+            return 0 <= b < BLOCKS
+
+        def is_group(q):
+            return 0 <= q < GROUPS
+
+        x_units = PASSES * SPANS
+        for step in range(FIRST_PRODUCT_STEP + GROUPS + 3):
+            summed, scaled, moved, coded = step, step - 1, step - 2, step - 3
+            made = step - FIRST_PRODUCT_STEP
+            squared, added, stored = made - 1, made - 2, made - 3
+
+            if is_group(stored):
+                turn_inverse_rms_back(stored)
+                fetch_inverse_rms(stored)
+            if is_block(moved):
+                transpose_filters(moved)
+            if is_group(added):
+                sum_over_heads(added)
+
+            if is_block(coded):
+                quantise_filters(coded)
+            if is_group(stored):
+                scale_and_store(stored)
+            if is_group(squared):
+                square_products(squared)
+            if is_group(added):
+                inverse_rms(added)
+            if is_block(summed):
+                filter_sum_squares(summed)
+                filter_scale(summed)
+            if is_block(moved):
+                regroup_filters(moved)
+            if is_block(scaled):
+                normalise_filters(scaled)
+            if is_group(made):
+                project(made)
+            unit, quantise = divmod(step - 2, 2)
+            if 0 <= unit < x_units:
+                if quantise:
+                    quantise_x(unit)
+                else:
+                    regroup_x(unit)

@@ -27,13 +27,10 @@ HEADS_PER_BANK = BANK // HEAD_DIM
 BANKS_PER_GROUP = HEADS // HEADS_PER_BANK
 
 BLOCKS = THIRDS * HEADS
-S_RUN = 4
-S_SPAN = P * S_RUN
-SPANS = POSITIONS // S_SPAN
 GROUPS_PER_THIRD = POSITIONS // P
 GROUPS = THIRDS * GROUPS_PER_THIRD
-BLOCK_STEPS = 4
-FIRST_PRODUCT_STEP = HEADS - 1 + BLOCK_STEPS - 1
+X_COLUMNS = 512
+X_UNITS = PASSES * POSITIONS // X_COLUMNS
 
 FLOPS = 2 * POSITIONS * CHANNELS * THIRDS * HEADS * HEAD_DIM
 
@@ -49,27 +46,23 @@ def tile_cosineattention_pa_kernel(tc, x, w_attn, out_0, out_1, out_2):
         keep = ctx.enter_context(tc.tile_pool(name="keep", bufs=1))
         x_stage = ctx.enter_context(tc.tile_pool(name="x_stage", bufs=2))
         w_stage = ctx.enter_context(tc.tile_pool(name="w_stage", bufs=3))
-        tiny = ctx.enter_context(tc.tile_pool(name="tiny", bufs=4))
+        tiny = ctx.enter_context(tc.tile_pool(name="tiny", bufs=3))
         norm = ctx.enter_context(tc.tile_pool(name="norm", bufs=3))
-        results = ctx.enter_context(tc.tile_pool(name="results", bufs=3))
+        results = ctx.enter_context(tc.tile_pool(name="results", bufs=4))
         psum = ctx.enter_context(tc.psum_pool(name="psum", bufs=2))
 
         identity = keep.tile([P, P], F32)
         zero_column = keep.tile([P, 1], F32)
         eps_column = keep.tile([P, 1], F32)
         table_warmer = keep.tile([P, 1], F32)
-        half_column = keep.tile([P, 1], F32)
-        minus_one_column = keep.tile([P, 1], F32)
+        half_pair = keep.tile([P, 2], F32)
+        minus_one_pair = keep.tile([P, 2], F32)
         x_raw = keep.tile([P, PASSES * PACK, POSITIONS], BF16)
         x_codes = keep.tile([P, PASSES, POSITIONS], U32, align_bytes=64)
         x_scales = keep.tile([P, PASSES, POSITIONS], U8, align_bytes=64)
         w_raw = keep.tile([P, BLOCKS, CHANNELS], BF16)
         w_codes = keep.tile([P, BLOCKS // HEADS_PER_BANK, PASSES, BANK], U32, align_bytes=64)
         w_scales = keep.tile([P, BLOCKS // HEADS_PER_BANK, PASSES, BANK], U8, align_bytes=64)
-
-        small_bank = psum.tile([P, 2, P], F32, tag="small", bufs=1)
-        head_sum_turned = small_bank[:, 0, :]
-        inv_rms_bank = small_bank[:, 1, :]
 
         sum_squares = {}
         filter_scales = {}
@@ -79,9 +72,8 @@ def tile_cosineattention_pa_kernel(tc, x, w_attn, out_0, out_1, out_2):
         grouped_x = {}
         products = {}
         squares = {}
-        inv_rms_turned = {}
+        head_sums = {}
         inv_rms = {}
-        result = {}
 
         def load_everything():
             for b in range(BLOCKS):
@@ -93,56 +85,61 @@ def tile_cosineattention_pa_kernel(tc, x, w_attn, out_0, out_1, out_2):
                     )
 
         def regroup_x(unit):
-            g, span = divmod(unit, SPANS)
-            grouped = x_stage.tile([P, S_RUN, P, PACK], BF16, align_bytes=64)
+            g, part = divmod(unit, POSITIONS // X_COLUMNS)
+            grouped = x_stage.tile([P, X_COLUMNS, PACK], BF16, align_bytes=64)
             nc.vector.tensor_copy(
                 out=grouped[:],
-                in_=x_raw[:, PACK * g : PACK * (g + 1), S_SPAN * span : S_SPAN * (span + 1)].rearrange(
-                    "p t (m q) -> p q m t", q=S_RUN
+                in_=x_raw[:, PACK * g : PACK * (g + 1), X_COLUMNS * part : X_COLUMNS * (part + 1)].rearrange(
+                    "p t s -> p s t"
                 ),
             )
             grouped_x[unit] = grouped
 
         def quantise_x(unit):
-            g, span = divmod(unit, SPANS)
-            columns = slice(S_SPAN * span, S_SPAN * (span + 1))
+            g, part = divmod(unit, POSITIONS // X_COLUMNS)
+            columns = slice(X_COLUMNS * part, X_COLUMNS * (part + 1))
             nc.vector.quantize_mx(
                 out=x_codes[:, g, columns].bitcast(FP8X4),
                 scales=x_scales[:, g, columns],
-                in_=grouped_x[unit][:].rearrange("p q m t -> p (q m t)"),
+                in_=grouped_x[unit][:].rearrange("p s t -> p (s t)"),
             )
 
         def filter_sum_squares(b):
+            pair, member = divmod(b, 2)
+            if member == 0:
+                sum_squares[pair] = tiny.tile([P, 2], F32, name="totals")
             unread = w_stage.tile([P, CHANNELS], BF16)
-            total = tiny.tile([P, 1], F32)
-            nc.scalar.activation(out=unread[:], in_=w_raw[:, b, :], func=ACT.Square, accum_out=total[:])
-            sum_squares[b] = total
+            nc.scalar.activation(
+                out=unread[:], in_=w_raw[:, b, :], func=ACT.Square, accum_out=sum_squares[pair][:, member : member + 1]
+            )
 
-        def filter_scale(b):
-            length = tiny.tile([P, 1], F32)
-            nc.gpsimd.tensor_tensor(out=length[:], in0=sum_squares[b][:], in1=half_column[:], op=ALU.pow)
-            padded = tiny.tile([P, 1], F32)
-            nc.gpsimd.tensor_scalar_add(out=padded[:], in0=length[:], scalar1=NORM_FLOOR)
-            scale = tiny.tile([P, 1], F32)
-            nc.gpsimd.tensor_tensor(out=scale[:], in0=padded[:], in1=minus_one_column[:], op=ALU.pow)
-            filter_scales[b] = scale
+        def filter_scale(pair):
+            lengths = tiny.tile([P, 2], F32)
+            nc.gpsimd.tensor_tensor(out=lengths[:], in0=sum_squares[pair][:], in1=half_pair[:], op=ALU.pow)
+            padded = tiny.tile([P, 2], F32)
+            nc.gpsimd.tensor_scalar_add(out=padded[:], in0=lengths[:], scalar1=NORM_FLOOR)
+            scales = tiny.tile([P, 2], F32)
+            nc.gpsimd.tensor_tensor(out=scales[:], in0=padded[:], in1=minus_one_pair[:], op=ALU.pow)
+            filter_scales[pair] = scales
 
         def normalise_filters(b):
+            pair, member = divmod(b, 2)
             wn = w_stage.tile([P, CHANNELS], BF16)
-            nc.vector.tensor_scalar_mul(out=wn[:], in0=w_raw[:, b, :], scalar1=filter_scales[b][:])
+            nc.vector.tensor_scalar_mul(
+                out=wn[:], in0=w_raw[:, b, :], scalar1=filter_scales[pair][:, member : member + 1]
+            )
             normed[b] = wn
 
         def transpose_filters(b):
             words = normed[b][:].bitcast(F32)
-            bank = psum.tile([P, PASSES * 2, P], F32, tag="turned", bufs=1)
+            bank = psum.tile([P, PASSES * 2, P], F32, tag="turned", bufs=2)
             for c in range(PASSES * 2):
                 nc.tensor.transpose(bank[:, c, :], words[:, P * c : P * (c + 1)], identity[:])
             turned[b] = bank
 
         def regroup_filters(b):
             grouped = w_stage.tile([P, PASSES, P, PACK], BF16, align_bytes=64)
-            copy = nc.scalar.copy if b < HEADS else nc.vector.tensor_copy
-            copy(
+            nc.scalar.copy(
                 out=grouped[:]
                 .rearrange("p g o t -> p (g o t)")
                 .bitcast(F32)
@@ -187,58 +184,43 @@ def tile_cosineattention_pa_kernel(tc, x, w_attn, out_0, out_1, out_2):
             squares[q] = sq
 
         def sum_over_heads(q):
-            for n in range(HEADS):
-                nc.tensor.matmul(
-                    out=head_sum_turned,
-                    lhsT=squares[q][:, HEAD_DIM * n : HEAD_DIM * (n + 1)],
-                    rhs=identity[:],
-                    is_transpose=True,
-                    start=(n == 0),
-                    stop=(n == HEADS - 1),
-                )
+            total = norm.tile([P, HEAD_DIM], F32)
+            nc.vector.tensor_reduce(
+                out=total[:],
+                in_=squares[q][:].rearrange("p (n d) -> p d n", n=HEADS),
+                axis=mybir.AxisListType.X,
+                op=ALU.add,
+            )
+            head_sums[q] = total
 
         def inverse_rms(q):
-            r_turned = norm.tile([P, P], F32)
-            nc.scalar.activation(
-                out=r_turned[:], in_=head_sum_turned, func=ACT.Abs_reciprocal_sqrt, scale=1.0 / HEADS, bias=eps_column[:]
-            )
-            inv_rms_turned[q] = r_turned
-
-        def turn_inverse_rms_back(q):
-            nc.tensor.transpose(inv_rms_bank, inv_rms_turned[q][:], identity[:])
-
-        def fetch_inverse_rms(q):
             r = norm.tile([P, HEAD_DIM], F32)
-            nc.scalar.copy(out=r[:], in_=inv_rms_bank)
+            nc.scalar.activation(
+                out=r[:], in_=head_sums[q][:], func=ACT.Abs_reciprocal_sqrt, scale=1.0 / HEADS, bias=eps_column[:]
+            )
             inv_rms[q] = r
 
         def scale_and_store(q):
             third, block = divmod(q, GROUPS_PER_THIRD)
-            span, run = divmod(block, S_RUN)
-            if run == 0:
-                result[0] = results.tile([P, HEADS, S_RUN, HEAD_DIM], F32, name="res")
-            res = result[0]
+            res = results.tile([P, HEADS, HEAD_DIM], F32)
             for h in range(BANKS_PER_GROUP):
                 heads = slice(HEADS_PER_BANK * h, HEADS_PER_BANK * (h + 1))
                 nc.vector.tensor_tensor(
-                    out=res[:, heads, run, :],
+                    out=res[:, heads, :],
                     in0=products[q][h][:].rearrange("p (n d) -> p n d", n=HEADS_PER_BANK),
                     in1=inv_rms[q][:].unsqueeze(1).to_broadcast([P, HEADS_PER_BANK, HEAD_DIM]),
                     op=ALU.mult,
                 )
-                if run == S_RUN - 1:
-                    nc.sync.dma_start(
-                        out=outs[third][heads, S_SPAN * span : S_SPAN * (span + 1), :].rearrange(
-                            "n (m q) d -> m n (q d)", q=S_RUN
-                        ),
-                        in_=res[:, heads, :, :].rearrange("m n q d -> m n (q d)"),
-                    )
+                nc.sync.dma_start(
+                    out=outs[third][heads, P * block : P * (block + 1), :].rearrange("n s d -> s n d"),
+                    in_=res[:, heads, :],
+                )
 
         load_everything()
         nc.vector.memset(zero_column[:], 0.0)
         nc.vector.tensor_scalar_add(out=eps_column[:], in0=zero_column[:], scalar1=EPS)
-        nc.vector.memset(half_column[:], 0.5)
-        nc.vector.memset(minus_one_column[:], -1.0)
+        nc.vector.memset(half_pair[:], 0.5)
+        nc.vector.memset(minus_one_pair[:], -1.0)
         nc.scalar.activation(out=table_warmer[:], in_=eps_column[:], func=ACT.Abs_reciprocal_sqrt)
         masks.make_identity(nc, identity[:])
 
@@ -248,31 +230,30 @@ def tile_cosineattention_pa_kernel(tc, x, w_attn, out_0, out_1, out_2):
         def is_group(q):
             return 0 <= q < GROUPS
 
-        x_units = PASSES * SPANS
-        for step in range(FIRST_PRODUCT_STEP + GROUPS + 3):
-            summed, scaled, moved, coded = step, step - 1, step - 2, step - 3
-            made = step - FIRST_PRODUCT_STEP
-            squared, added, stored = made - 1, made - 2, made - 3
+        last_block_stage = 4
+        first_product_step = HEADS - 1 + last_block_stage
+        last_group_stage = 3
+        for step in range(first_product_step + GROUPS + last_group_stage):
+            summed, scaled, moved, coded = step, step - 2, step - 3, step - last_block_stage
+            made = step - first_product_step
+            squared, added, stored = made - 1, made - 2, made - last_group_stage
 
-            if is_group(stored):
-                turn_inverse_rms_back(stored)
-                fetch_inverse_rms(stored)
             if is_block(moved):
                 transpose_filters(moved)
             if is_group(added):
                 sum_over_heads(added)
-
-            if is_block(coded):
-                quantise_filters(coded)
             if is_group(stored):
                 scale_and_store(stored)
+            if is_block(coded):
+                quantise_filters(coded)
             if is_group(squared):
                 square_products(squared)
             if is_group(added):
                 inverse_rms(added)
             if is_block(summed):
                 filter_sum_squares(summed)
-                filter_scale(summed)
+                if summed % 2 == 1:
+                    filter_scale(summed // 2)
             if is_block(moved):
                 regroup_filters(moved)
             if is_block(scaled):
@@ -280,7 +261,7 @@ def tile_cosineattention_pa_kernel(tc, x, w_attn, out_0, out_1, out_2):
             if is_group(made):
                 project(made)
             unit, quantise = divmod(step - 2, 2)
-            if 0 <= unit < x_units:
+            if 0 <= unit < X_UNITS:
                 if quantise:
                     quantise_x(unit)
                 else:

@@ -25,6 +25,7 @@ NORM_FLOOR = EPS * math.sqrt(CHANNELS)
 BANK = 512
 HEADS_PER_BANK = BANK // HEAD_DIM
 BANKS_PER_GROUP = HEADS // HEADS_PER_BANK
+FOLDS = 3
 
 BLOCKS = THIRDS * HEADS
 GROUPS_PER_THIRD = POSITIONS // P
@@ -48,7 +49,7 @@ def tile_cosineattention_pa_kernel(tc, x, w_attn, out_0, out_1, out_2):
         w_stage = ctx.enter_context(tc.tile_pool(name="w_stage", bufs=3))
         tiny = ctx.enter_context(tc.tile_pool(name="tiny", bufs=3))
         norm = ctx.enter_context(tc.tile_pool(name="norm", bufs=3))
-        results = ctx.enter_context(tc.tile_pool(name="results", bufs=4))
+        results = ctx.enter_context(tc.tile_pool(name="results", bufs=6))
         psum = ctx.enter_context(tc.psum_pool(name="psum", bufs=2))
 
         identity = keep.tile([P, P], F32)
@@ -72,7 +73,6 @@ def tile_cosineattention_pa_kernel(tc, x, w_attn, out_0, out_1, out_2):
         grouped_x = {}
         products = {}
         squares = {}
-        head_sums = {}
         inv_rms = {}
 
         def load_everything():
@@ -183,38 +183,34 @@ def tile_cosineattention_pa_kernel(tc, x, w_attn, out_0, out_1, out_2):
                 nc.scalar.activation(out=sq[:, BANK * h : BANK * (h + 1)], in_=products[q][h][:], func=ACT.Square)
             squares[q] = sq
 
-        def sum_over_heads(q):
-            total = norm.tile([P, HEAD_DIM], F32)
-            nc.vector.tensor_reduce(
-                out=total[:],
-                in_=squares[q][:].rearrange("p (n d) -> p d n", n=HEADS),
-                axis=mybir.AxisListType.X,
-                op=ALU.add,
+        def fold_heads(q, level):
+            width = HEADS * HEAD_DIM >> (level + 1)
+            folded = norm.tile([P, width], F32, name="folded%d" % level)
+            nc.vector.tensor_tensor(
+                out=folded[:], in0=squares[q][:, :width], in1=squares[q][:, width : 2 * width], op=ALU.add
             )
-            head_sums[q] = total
+            squares[q] = folded
 
         def inverse_rms(q):
             r = norm.tile([P, HEAD_DIM], F32)
             nc.scalar.activation(
-                out=r[:], in_=head_sums[q][:], func=ACT.Abs_reciprocal_sqrt, scale=1.0 / HEADS, bias=eps_column[:]
+                out=r[:], in_=squares[q][:], func=ACT.Abs_reciprocal_sqrt, scale=1.0 / HEADS, bias=eps_column[:]
             )
             inv_rms[q] = r
 
-        def scale_and_store(q):
+        def scale_and_store(q, h):
             third, block = divmod(q, GROUPS_PER_THIRD)
-            res = results.tile([P, HEADS, HEAD_DIM], F32)
-            for h in range(BANKS_PER_GROUP):
-                heads = slice(HEADS_PER_BANK * h, HEADS_PER_BANK * (h + 1))
-                nc.vector.tensor_tensor(
-                    out=res[:, heads, :],
-                    in0=products[q][h][:].rearrange("p (n d) -> p n d", n=HEADS_PER_BANK),
-                    in1=inv_rms[q][:].unsqueeze(1).to_broadcast([P, HEADS_PER_BANK, HEAD_DIM]),
-                    op=ALU.mult,
-                )
-                nc.sync.dma_start(
-                    out=outs[third][heads, P * block : P * (block + 1), :].rearrange("n s d -> s n d"),
-                    in_=res[:, heads, :],
-                )
+            heads = slice(HEADS_PER_BANK * h, HEADS_PER_BANK * (h + 1))
+            res = results.tile([P, HEADS_PER_BANK, HEAD_DIM], F32)
+            nc.vector.tensor_tensor(
+                out=res[:],
+                in0=products[q][h][:].rearrange("p (n d) -> p n d", n=HEADS_PER_BANK),
+                in1=inv_rms[q][:].unsqueeze(1).to_broadcast([P, HEADS_PER_BANK, HEAD_DIM]),
+                op=ALU.mult,
+            )
+            nc.sync.dma_start(
+                out=outs[third][heads, P * block : P * (block + 1), :].rearrange("n s d -> s n d"), in_=res[:]
+            )
 
         load_everything()
         nc.vector.memset(zero_column[:], 0.0)
@@ -240,10 +236,11 @@ def tile_cosineattention_pa_kernel(tc, x, w_attn, out_0, out_1, out_2):
 
             if is_block(moved):
                 transpose_filters(moved)
-            if is_group(added):
-                sum_over_heads(added)
-            if is_group(stored):
-                scale_and_store(stored)
+            for level in range(FOLDS):
+                if is_group(added):
+                    fold_heads(added, level)
+                if is_group(stored) and level < BANKS_PER_GROUP:
+                    scale_and_store(stored, level)
             if is_block(coded):
                 quantise_filters(coded)
             if is_group(squared):

@@ -25,7 +25,6 @@ NORM_FLOOR = EPS * math.sqrt(CHANNELS)
 BANK = 512
 HEADS_PER_BANK = BANK // HEAD_DIM
 BANKS_PER_GROUP = HEADS // HEADS_PER_BANK
-FOLDS = 3
 
 BLOCKS = THIRDS * HEADS
 GROUPS_PER_THIRD = POSITIONS // P
@@ -73,6 +72,8 @@ def tile_cosineattention_pa_kernel(tc, x, w_attn, out_0, out_1, out_2):
         grouped_x = {}
         products = {}
         squares = {}
+        folded_squares = {}
+        head_sums = {}
         inv_rms = {}
 
         def load_everything():
@@ -132,14 +133,15 @@ def tile_cosineattention_pa_kernel(tc, x, w_attn, out_0, out_1, out_2):
 
         def transpose_filters(b):
             words = normed[b][:].bitcast(F32)
-            bank = psum.tile([P, PASSES * 2, P], F32, tag="turned", bufs=2)
+            bank = psum.tile([P, PASSES * 2, P], F32, tag="turned", bufs=1)
             for c in range(PASSES * 2):
                 nc.tensor.transpose(bank[:, c, :], words[:, P * c : P * (c + 1)], identity[:])
             turned[b] = bank
 
         def regroup_filters(b):
             grouped = w_stage.tile([P, PASSES, P, PACK], BF16, align_bytes=64)
-            nc.scalar.copy(
+            copy = nc.scalar.copy if b < HEADS or b % 2 == 1 else nc.vector.tensor_copy
+            copy(
                 out=grouped[:]
                 .rearrange("p g o t -> p (g o t)")
                 .bitcast(F32)
@@ -183,18 +185,27 @@ def tile_cosineattention_pa_kernel(tc, x, w_attn, out_0, out_1, out_2):
                 nc.scalar.activation(out=sq[:, BANK * h : BANK * (h + 1)], in_=products[q][h][:], func=ACT.Square)
             squares[q] = sq
 
-        def fold_heads(q, level):
-            width = HEADS * HEAD_DIM >> (level + 1)
-            folded = norm.tile([P, width], F32, name="folded%d" % level)
-            nc.vector.tensor_tensor(
-                out=folded[:], in0=squares[q][:, :width], in1=squares[q][:, width : 2 * width], op=ALU.add
-            )
-            squares[q] = folded
+        def fold_heads(q):
+            folded = norm.tile([P, BANK], F32)
+            nc.vector.tensor_tensor(out=folded[:], in0=squares[q][:, :BANK], in1=squares[q][:, BANK:], op=ALU.add)
+            folded_squares[q] = folded
+
+        def add_folded_heads(q):
+            total = psum.tile([P, HEAD_DIM], F32, tag="head_sum", bufs=1)
+            for n in range(HEADS_PER_BANK):
+                nc.tensor.matmul(
+                    out=total[:],
+                    lhsT=identity[:],
+                    rhs=folded_squares[q][:, HEAD_DIM * n : HEAD_DIM * (n + 1)],
+                    start=(n == 0),
+                    stop=(n == HEADS_PER_BANK - 1),
+                )
+            head_sums[q] = total
 
         def inverse_rms(q):
             r = norm.tile([P, HEAD_DIM], F32)
             nc.scalar.activation(
-                out=r[:], in_=squares[q][:], func=ACT.Abs_reciprocal_sqrt, scale=1.0 / HEADS, bias=eps_column[:]
+                out=r[:], in_=head_sums[q][:], func=ACT.Abs_reciprocal_sqrt, scale=1.0 / HEADS, bias=eps_column[:]
             )
             inv_rms[q] = r
 
@@ -234,23 +245,25 @@ def tile_cosineattention_pa_kernel(tc, x, w_attn, out_0, out_1, out_2):
             made = step - first_product_step
             squared, added, stored = made - 1, made - 2, made - last_group_stage
 
-            if is_block(moved):
-                transpose_filters(moved)
-            for level in range(FOLDS):
-                if is_group(added):
-                    fold_heads(added, level)
-                if is_group(stored) and level < BANKS_PER_GROUP:
-                    scale_and_store(stored, level)
+            if is_group(added):
+                fold_heads(added)
+            if is_group(stored):
+                for h in range(BANKS_PER_GROUP):
+                    scale_and_store(stored, h)
             if is_block(coded):
                 quantise_filters(coded)
-            if is_group(squared):
-                square_products(squared)
+            if is_block(moved):
+                transpose_filters(moved)
             if is_group(added):
-                inverse_rms(added)
+                add_folded_heads(added)
             if is_block(summed):
                 filter_sum_squares(summed)
                 if summed % 2 == 1:
                     filter_scale(summed // 2)
+            if is_group(squared):
+                square_products(squared)
+            if is_group(added):
+                inverse_rms(added)
             if is_block(moved):
                 regroup_filters(moved)
             if is_block(scaled):

import math
from contextlib import ExitStack

import concourse.masks as masks
import concourse.mybir as mybir

F32 = mybir.dt.float32
BF16 = mybir.dt.bfloat16
U32 = mybir.dt.uint32
U8 = mybir.dt.uint8
FP8X4 = mybir.dt.float8_e4m3fn_x4
ACT = mybir.ActivationFunctionType
ALU = mybir.AluOpType

P = 128
PACK = 4
CHANNELS = 1024
PASSES = CHANNELS // (P * PACK)
POSITIONS = 1024
HEADS = 8
HEAD_DIM = 128
THIRDS = 3
EPS = 1e-4
NORM_FLOOR = EPS * math.sqrt(CHANNELS)
BANK = 512
HEADS_PER_BANK = BANK // HEAD_DIM
BANKS_PER_GROUP = HEADS // HEADS_PER_BANK

BLOCKS = THIRDS * HEADS
GROUPS_PER_THIRD = POSITIONS // P
GROUPS = THIRDS * GROUPS_PER_THIRD
X_COLUMNS = 512
X_UNITS = PASSES * POSITIONS // X_COLUMNS

FLOPS = 2 * POSITIONS * CHANNELS * THIRDS * HEADS * HEAD_DIM


def tile_cosineattention_pa_kernel(tc, x, w_attn, out_0, out_1, out_2):
    nc = tc.nc
    x_rows = x.rearrange("b c h w -> (b c) (h w)")
    w_rows = w_attn.rearrange("o i a b -> o (i a b)")
    outs = [o.rearrange("b n s d -> (b n) s d") for o in (out_0, out_1, out_2)]

    with ExitStack() as ctx:
        ctx.enter_context(tc.manual_schedule())
        keep = ctx.enter_context(tc.tile_pool(name="keep", bufs=1))
        x_stage = ctx.enter_context(tc.tile_pool(name="x_stage", bufs=2))
        w_stage = ctx.enter_context(tc.tile_pool(name="w_stage", bufs=3))
        tiny = ctx.enter_context(tc.tile_pool(name="tiny", bufs=3))
        norm = ctx.enter_context(tc.tile_pool(name="norm", bufs=3))
        results = ctx.enter_context(tc.tile_pool(name="results", bufs=6))
        psum = ctx.enter_context(tc.psum_pool(name="psum", bufs=2))

        identity = keep.tile([P, P], F32)
        zero_column = keep.tile([P, 1], F32)
        eps_column = keep.tile([P, 1], F32)
        table_warmer = keep.tile([P, 1], F32)
        half_pair = keep.tile([P, 2], F32)
        minus_one_pair = keep.tile([P, 2], F32)
        x_raw = keep.tile([P, PASSES * PACK, POSITIONS], BF16)
        x_codes = keep.tile([P, PASSES, POSITIONS], U32, align_bytes=64)
        x_scales = keep.tile([P, PASSES, POSITIONS], U8, align_bytes=64)
        w_raw = keep.tile([P, BLOCKS, CHANNELS], BF16)
        w_codes = keep.tile([P, BLOCKS // HEADS_PER_BANK, PASSES, BANK], U32, align_bytes=64)
        w_scales = keep.tile([P, BLOCKS // HEADS_PER_BANK, PASSES, BANK], U8, align_bytes=64)

        sum_squares = {}
        filter_scales = {}
        normed = {}
        turned = {}
        grouped_w = {}
        grouped_x = {}
        products = {}
        squares = {}
        folded_squares = {}
        head_sums = {}
        inv_rms = {}

        def load_everything():
            for b in range(BLOCKS):
                nc.sync.dma_start(out=w_raw[:, b, :], in_=w_rows[P * b : P * (b + 1), :])
                if b < PASSES * 2:
                    nc.sync.dma_start(
                        out=x_raw[:, 2 * b : 2 * b + 2, :],
                        in_=x_rows[2 * P * b : 2 * P * (b + 1), :].rearrange("(p e) s -> p e s", e=2),
                    )

        def regroup_x(unit):
            g, part = divmod(unit, POSITIONS // X_COLUMNS)
            grouped = x_stage.tile([P, X_COLUMNS, PACK], BF16, align_bytes=64)
            nc.vector.tensor_copy(
                out=grouped[:],
                in_=x_raw[:, PACK * g : PACK * (g + 1), X_COLUMNS * part : X_COLUMNS * (part + 1)].rearrange(
                    "p t s -> p s t"
                ),
            )
            grouped_x[unit] = grouped

        def quantise_x(unit):
            g, part = divmod(unit, POSITIONS // X_COLUMNS)
            columns = slice(X_COLUMNS * part, X_COLUMNS * (part + 1))
            nc.vector.quantize_mx(
                out=x_codes[:, g, columns].bitcast(FP8X4),
                scales=x_scales[:, g, columns],
                in_=grouped_x[unit][:].rearrange("p s t -> p (s t)"),
            )

        def filter_sum_squares(b):
            pair, member = divmod(b, 2)
            if member == 0:
                sum_squares[pair] = tiny.tile([P, 2], F32, name="totals")
            unread = w_stage.tile([P, CHANNELS], BF16)
            nc.scalar.activation(
                out=unread[:], in_=w_raw[:, b, :], func=ACT.Square, accum_out=sum_squares[pair][:, member : member + 1]
            )

        def filter_scale(pair):
            lengths = tiny.tile([P, 2], F32)
            nc.gpsimd.tensor_tensor(out=lengths[:], in0=sum_squares[pair][:], in1=half_pair[:], op=ALU.pow)
            padded = tiny.tile([P, 2], F32)
            nc.gpsimd.tensor_scalar_add(out=padded[:], in0=lengths[:], scalar1=NORM_FLOOR)
            scales = tiny.tile([P, 2], F32)
            nc.gpsimd.tensor_tensor(out=scales[:], in0=padded[:], in1=minus_one_pair[:], op=ALU.pow)
            filter_scales[pair] = scales

        def normalise_filters(b):
            pair, member = divmod(b, 2)
            wn = w_stage.tile([P, CHANNELS], BF16)
            nc.vector.tensor_scalar_mul(
                out=wn[:], in0=w_raw[:, b, :], scalar1=filter_scales[pair][:, member : member + 1]
            )
            normed[b] = wn

        def transpose_filters(b):
            words = normed[b][:].bitcast(F32)
            bank = psum.tile([P, PASSES * 2, P], F32, tag="turned", bufs=1)
            for c in range(PASSES * 2):
                nc.tensor.transpose(bank[:, c, :], words[:, P * c : P * (c + 1)], identity[:])
            turned[b] = bank

        def regroup_filters(b):
            grouped = w_stage.tile([P, PASSES, P, PACK], BF16, align_bytes=64)
            copy = nc.scalar.copy if b < HEADS or b % 2 == 1 else nc.vector.tensor_copy
            copy(
                out=grouped[:]
                .rearrange("p g o t -> p (g o t)")
                .bitcast(F32)
                .rearrange("p (g o u) -> p g o u", g=PASSES, u=2),
                in_=turned[b][:].rearrange("p (g u) o -> p g o u", u=2),
            )
            grouped_w[b] = grouped

        def quantise_filters(b):
            bank, head = divmod(b, HEADS_PER_BANK)
            columns = slice(HEAD_DIM * head, HEAD_DIM * (head + 1))
            for g in range(PASSES):
                nc.vector.quantize_mx(
                    out=w_codes[:, bank, g, columns].bitcast(FP8X4),
                    scales=w_scales[:, bank, g, columns],
                    in_=grouped_w[b][:, g].rearrange("p o t -> p (o t)"),
                )

        def project(q):
            third, block = divmod(q, GROUPS_PER_THIRD)
            columns = slice(P * block, P * (block + 1))
            banks = []
            for h in range(BANKS_PER_GROUP):
                bank = psum.tile([P, BANK], F32, tag="product", bufs=6)
                for g in range(PASSES):
                    nc.tensor.matmul_mx(
                        out=bank[:],
                        lhsT=x_codes[:, g, columns].bitcast(FP8X4),
                        lhsT_scale=x_scales[:, g, columns],
                        rhs=w_codes[:, BANKS_PER_GROUP * third + h, g, :].bitcast(FP8X4),
                        rhs_scale=w_scales[:, BANKS_PER_GROUP * third + h, g, :],
                        start=(g == 0),
                        stop=(g == PASSES - 1),
                    )
                banks.append(bank)
            products[q] = banks

        def square_products(q):
            sq = norm.tile([P, HEADS * HEAD_DIM], F32)
            for h in range(BANKS_PER_GROUP):
                nc.scalar.activation(out=sq[:, BANK * h : BANK * (h + 1)], in_=products[q][h][:], func=ACT.Square)
            squares[q] = sq

        def fold_heads(q):
            folded = norm.tile([P, BANK], F32)
            nc.vector.tensor_tensor(out=folded[:], in0=squares[q][:, :BANK], in1=squares[q][:, BANK:], op=ALU.add)
            folded_squares[q] = folded

        def add_folded_heads(q):
            total = psum.tile([P, HEAD_DIM], F32, tag="head_sum", bufs=1)
            for n in range(HEADS_PER_BANK):
                nc.tensor.matmul(
                    out=total[:],
                    lhsT=identity[:],
                    rhs=folded_squares[q][:, HEAD_DIM * n : HEAD_DIM * (n + 1)],
                    start=(n == 0),
                    stop=(n == HEADS_PER_BANK - 1),
                )
            head_sums[q] = total

        def inverse_rms(q):
            r = norm.tile([P, HEAD_DIM], F32)
            nc.scalar.activation(
                out=r[:], in_=head_sums[q][:], func=ACT.Abs_reciprocal_sqrt, scale=1.0 / HEADS, bias=eps_column[:]
            )
            inv_rms[q] = r

        def scale_and_store(q, h):
            third, block = divmod(q, GROUPS_PER_THIRD)
            heads = slice(HEADS_PER_BANK * h, HEADS_PER_BANK * (h + 1))
            res = results.tile([P, HEADS_PER_BANK, HEAD_DIM], F32)
            nc.vector.tensor_tensor(
                out=res[:],
                in0=products[q][h][:].rearrange("p (n d) -> p n d", n=HEADS_PER_BANK),
                in1=inv_rms[q][:].unsqueeze(1).to_broadcast([P, HEADS_PER_BANK, HEAD_DIM]),
                op=ALU.mult,
            )
            nc.sync.dma_start(
                out=outs[third][heads, P * block : P * (block + 1), :].rearrange("n s d -> s n d"), in_=res[:]
            )

        load_everything()
        nc.vector.memset(zero_column[:], 0.0)
        nc.vector.tensor_scalar_add(out=eps_column[:], in0=zero_column[:], scalar1=EPS)
        nc.vector.memset(half_pair[:], 0.5)
        nc.vector.memset(minus_one_pair[:], -1.0)
        nc.scalar.activation(out=table_warmer[:], in_=eps_column[:], func=ACT.Abs_reciprocal_sqrt)
        masks.make_identity(nc, identity[:])

        def is_block(b):
            return 0 <= b < BLOCKS

        def is_group(q):
            return 0 <= q < GROUPS

        last_block_stage = 4
        first_product_step = HEADS - 1 + last_block_stage
        last_group_stage = 3
        for step in range(first_product_step + GROUPS + last_group_stage):
            summed, scaled, moved, coded = step, step - 2, step - 3, step - last_block_stage
            made = step - first_product_step
            squared, added, stored = made - 1, made - 2, made - last_group_stage

            if is_group(added):
                fold_heads(added)
            if is_group(stored):
                for h in range(BANKS_PER_GROUP):
                    scale_and_store(stored, h)
            if is_block(coded):
                quantise_filters(coded)
            if is_block(moved):
                transpose_filters(moved)
            if is_group(added):
                add_folded_heads(added)
            if is_block(summed):
                filter_sum_squares(summed)
                if summed % 2 == 1:
                    filter_scale(summed // 2)
            if is_group(squared):
                square_products(squared)
            if is_group(added):
                inverse_rms(added)
            if is_block(moved):
                regroup_filters(moved)
            if is_block(scaled):
                normalise_filters(scaled)
            if is_group(made):
                project(made)
            unit, quantise = divmod(step - 2, 2)
            if 0 <= unit < X_UNITS:
                if quantise:
                    quantise_x(unit)
                else:
                    regroup_x(unit)
